import numpy as np
import ml_dtypes


def mxq(x, axis, fmt="e4m3"):
    dtype, down = {"e4m3": (ml_dtypes.float8_e4m3fn, 7), "e5m2": (ml_dtypes.float8_e5m2, 14)}[fmt]
    v = np.moveaxis(np.asarray(x, np.float32).astype(ml_dtypes.bfloat16).astype(np.float64), axis, -1)
    blocks = v.reshape(v.shape[:-1] + (-1, 32))
    amax = np.abs(blocks).max(-1, keepdims=True)
    byte = np.maximum(np.where(amax > 0, np.frexp(amax)[1] - 1 + 127, 0) - down, 1)
    scale = np.exp2(byte - 127.0)
    codes = (blocks / scale).astype(np.float32).astype(dtype).astype(np.float64)
    return np.moveaxis((codes * scale).reshape(v.shape), -1, axis)


WIDE = False


def mx_kscale(k):
    if not WIDE:
        return np.ones(k)
    levels = np.array([10, -10, 5, -5, 0])
    if k % 512:
        return np.exp2(np.random.permutation(np.resize(levels, k // 32))).repeat(32)
    a = np.empty((k // 512, 16))
    for p in range(k // 512):
        a[p, :8] = np.random.permutation(np.resize(levels, 8))
        for g in range(8):
            far = levels[np.abs(levels - a[p, g]) >= 10]
            a[p, g + 8] = far[np.random.randint(len(far))]
    return np.exp2(a.ravel()).repeat(32)


BF16 = ml_dtypes.bfloat16


def bf(x):
    return np.asarray(x, np.float32).astype(BF16)


def f64(x):
    return np.asarray(x).astype(np.float64)


N, DB, DV, DL, DC, T, DO = 8192, 500, 500, 256, 128, 12, 256
KB, KV = DB + T, DV + T
LN_EPS = 1e-5
ERF_TERMS = 100


def erf(v):
    a = np.clip(v, -6.0, 6.0)
    term = a.copy()
    tot = a.copy()
    for n in range(1, ERF_TERMS):
        term = term * (2.0 * a * a) / (2.0 * n + 1.0)
        tot = tot + term
    return 2.0 / np.sqrt(np.pi) * np.exp(-a * a) * tot


def gelu_erf(v):
    return 0.5 * v * (1.0 + erf(v / np.sqrt(2.0)))


def t2v(t, w0, w, b):
    v0 = w0 * t + b[0]
    v = np.sin(w * t[:, None] + b[1:])
    return np.concatenate([v0[:, None], v], axis=-1)


def branch(z, gamma, beta, W):
    mu = z.mean(-1, keepdims=True)
    var = np.square(z - mu).mean(-1, keepdims=True)
    zn = (z - mu) / np.sqrt(var + LN_EPS) * gamma + beta
    return gelu_erf(mxq(zn, 1, "e4m3") @ mxq(W, 0, "e4m3"))


def rows(d):
    return np.random.standard_normal((N, d)) * (0.5 + np.random.uniform(size=(N, 1))) + 0.3 * np.random.standard_normal((N, 1))


def setup_inputs():
    sb, sv = mx_kscale(KB), mx_kscale(KV)
    return {"x_bill": bf(rows(DB)), "ts_bill": bf(np.random.uniform(size=N)),
            "x_bill_version": bf(rows(DV)), "ts_bill_version": bf(np.random.uniform(size=N)),
            "w0": bf(3.0 + 0.5 * np.random.standard_normal(1)),
            "w": bf(3.0 * np.random.standard_normal(T - 1)),
            "b": bf(1.5 + 0.5 * np.random.standard_normal(T)),
            "gamma_bill": bf((1.0 + 0.1 * np.random.standard_normal(KB)) * sb),
            "beta_bill": bf(0.1 * np.random.standard_normal(KB) * sb),
            "W_bill": bf(np.random.standard_normal((KB, DO)) * np.sqrt(2.0 / KB) / sb[:, None]),
            "gamma_bill_version": bf((1.0 + 0.1 * np.random.standard_normal(KV)) * sv),
            "beta_bill_version": bf(0.1 * np.random.standard_normal(KV) * sv),
            "W_bill_version": bf(np.random.standard_normal((KV, DO)) * np.sqrt(2.0 / KV) / sv[:, None])}


def reference(x_bill, ts_bill, x_bill_version, ts_bill_version, w0, w, b,
              gamma_bill, beta_bill, W_bill, gamma_bill_version, beta_bill_version, W_bill_version):
    w0, w, b = f64(w0), f64(w), f64(b)
    zb = np.concatenate([f64(x_bill), t2v(f64(ts_bill), w0, w, b)], axis=1)
    zv = np.concatenate([f64(x_bill_version), t2v(f64(ts_bill_version), w0, w, b)], axis=1)
    out_bill = branch(zb, f64(gamma_bill), f64(beta_bill), f64(W_bill))
    out_bv = branch(zv, f64(gamma_bill_version), f64(beta_bill_version), f64(W_bill_version))
    return np.stack([out_bill, out_bv], axis=0)

@@ -1,0 +1,308 @@
+import math
+from contextlib import ExitStack
+
+import concourse.mybir as mybir
+from concourse.masks import make_identity
+
+F32 = mybir.dt.float32
+BF16 = mybir.dt.bfloat16
+U32 = mybir.dt.uint32
+U8 = mybir.dt.uint8
+FP8X4 = mybir.dt.float8_e4m3fn_x4
+ALU = mybir.AluOpType
+ACT = mybir.ActivationFunctionType
+
+P = 128
+ROWS = 8192
+RAW = 500
+T2V = 12
+K = RAW + T2V
+PACK = 4
+D_OUT = 256
+KINDS = 2
+TILES = ROWS // P
+GROUP = 4
+GROUPS = TILES // GROUP
+LN_EPS = 1e-5
+ROUND_MAGIC = 12582912.0
+RAW_PARTS = RAW // PACK
+T2V_PARTS = T2V // PACK
+SCALAR_SHARE = 2
+LOAD_AHEAD = 6
+STATS_AHEAD = 4
+NORM_AHEAD = 2
+
+FLOPS = 2 * KINDS * ROWS * K * D_OUT
+
+
+def tile_featureprojector_pa_t_kernel(
+    tc,
+    x_bill,
+    ts_bill,
+    x_bill_version,
+    ts_bill_version,
+    w0,
+    w,
+    b,
+    gamma_bill,
+    beta_bill,
+    W_bill,
+    gamma_bill_version,
+    beta_bill_version,
+    W_bill_version,
+    out,
+):
+    nc = tc.nc
+    xs = [x_bill, x_bill_version]
+    stamps = [ts_bill, ts_bill_version]
+    weights = [W_bill, W_bill_version]
+    column_vectors = [gamma_bill, beta_bill, gamma_bill_version, beta_bill_version]
+
+    with ExitStack() as ctx:
+        keep = ctx.enter_context(tc.tile_pool(name="keep", bufs=1))
+        x_pool = ctx.enter_context(tc.tile_pool(name="x_pool", bufs=LOAD_AHEAD - NORM_AHEAD + 2))
+        small = ctx.enter_context(tc.tile_pool(name="small", bufs=STATS_AHEAD - NORM_AHEAD + 2))
+        u_pool = ctx.enter_context(tc.tile_pool(name="u_pool", bufs=NORM_AHEAD + 2))
+        q_pool = ctx.enter_context(tc.tile_pool(name="q_pool", bufs=3))
+        o_pool = ctx.enter_context(tc.tile_pool(name="o_pool", bufs=3))
+        psum_t = ctx.enter_context(tc.psum_pool(name="psum_t", bufs=6))
+        psum_o = ctx.enter_context(tc.psum_pool(name="psum_o", bufs=2))
+
+        ts_bf = keep.tile([P, KINDS, TILES], BF16, name="ts_bf")
+        for kind in range(KINDS):
+            nc.sync.dma_start(out=ts_bf[:, kind, :], in_=stamps[kind].rearrange("(p t) -> p t", t=TILES))
+        w0_bf = keep.tile([P, 1], BF16, name="w0_bf")
+        w_bf = keep.tile([P, T2V - 1], BF16, name="w_bf")
+        b_bf = keep.tile([P, T2V], BF16, name="b_bf")
+        nc.sync.dma_start(out=w0_bf[:], in_=w0.partition_broadcast(P))
+        nc.sync.dma_start(out=w_bf[:], in_=w.partition_broadcast(P))
+        nc.sync.dma_start(out=b_bf[:], in_=b.partition_broadcast(P))
+
+        def load_group(g):
+            kind, first = divmod(g, GROUPS)
+            first *= GROUP
+            x_sb = x_pool.tile([P, GROUP, RAW], BF16, name="x_sb")
+            rows = xs[kind].rearrange("(p t) k -> p t k", t=TILES)
+            nc.sync.dma_start(out=x_sb[:], in_=rows[:, first : first + GROUP, :])
+            return x_sb
+
+        x_tiles = {0: load_group(0)}
+
+        vec_bf = keep.tile([P, len(column_vectors), 16], BF16, name="vec_bf")
+        for v in range(len(column_vectors)):
+            nc.sync.dma_start(
+                out=vec_bf[:, v, 0:PACK],
+                in_=column_vectors[v].rearrange("(p t) -> p t", t=PACK),
+            )
+        w_raw = []
+        for kind in range(KINDS):
+            raw = keep.tile([P, PACK, D_OUT], BF16, name="w_raw%d" % kind)
+            nc.sync.dma_start(out=raw[:], in_=weights[kind].rearrange("(p t) n -> p t n", t=PACK))
+            w_raw.append(raw)
+        for g in range(1, LOAD_AHEAD - STATS_AHEAD):
+            x_tiles[g] = load_group(g)
+
+        identity = keep.tile([P, P], F32, name="identity")
+        make_identity(nc, identity[:])
+        neg_half = keep.tile([P, GROUP, 1], F32, name="neg_half")
+        nc.gpsimd.memset(neg_half[:], -0.5)
+
+        slope = keep.tile([P, T2V], F32, name="slope")
+        phase = keep.tile([P, T2V], F32, name="phase")
+        turn = 1.0 / (2.0 * math.pi)
+        nc.vector.tensor_copy(out=slope[:, 0:1], in_=w0_bf[:])
+        nc.vector.tensor_copy(out=phase[:, 0:1], in_=b_bf[:, 0:1])
+        nc.vector.tensor_scalar(out=slope[:, 1:T2V], in0=w_bf[:], scalar1=turn, scalar2=None, op0=ALU.mult)
+        nc.vector.tensor_scalar(out=phase[:, 1:T2V], in0=b_bf[:, 1:T2V], scalar1=turn, scalar2=None, op0=ALU.mult)
+        all_tiles = KINDS * TILES
+        feat = keep.tile([P, T2V, all_tiles], F32, name="feat")
+        for j in range(T2V):
+            nc.scalar.activation(
+                out=feat[:, j, :],
+                in_=ts_bf[:].rearrange("p a t -> p (a t)"),
+                func=ACT.Identity,
+                scale=slope[:, j : j + 1],
+                bias=phase[:, j : j + 1],
+            )
+        sines = feat[:, 1:T2V, :]
+        whole = keep.tile([P, T2V - 1, all_tiles], F32, name="whole")
+        nc.vector.tensor_scalar(
+            out=whole[:], in0=sines, scalar1=ROUND_MAGIC, scalar2=ROUND_MAGIC, op0=ALU.add, op1=ALU.subtract
+        )
+        nc.vector.tensor_tensor(out=sines, in0=sines, in1=whole[:], op=ALU.subtract)
+        nc.scalar.activation(out=sines, in_=sines, func=ACT.Sin, scale=2.0 * math.pi)
+
+        squares = keep.tile([P, T2V, all_tiles], F32, name="squares")
+        nc.scalar.activation(out=squares[:], in_=feat[:], func=ACT.Square)
+        feat_sum = keep.tile([P, all_tiles], F32, name="feat_sum")
+        feat_sq = keep.tile([P, all_tiles], F32, name="feat_sq")
+        nc.vector.tensor_reduce(
+            out=feat_sum[:], in_=feat[:].rearrange("p j g -> p g j"), axis=mybir.AxisListType.X, op=ALU.add
+        )
+        nc.vector.tensor_reduce(
+            out=feat_sq[:], in_=squares[:].rearrange("p j g -> p g j"), axis=mybir.AxisListType.X, op=ALU.add
+        )
+        stats = keep.tile([P, all_tiles, 9], F32, name="stats")
+        feat_stats = stats[:, :, 6:9]
+        nc.vector.memset(feat_stats[:, :, 0:1], float(T2V))
+        nc.vector.tensor_scalar(
+            out=feat_stats[:, :, 1:2], in0=feat_sum[:].unsqueeze(2), scalar1=1.0 / T2V, scalar2=None, op0=ALU.mult
+        )
+        nc.vector.tensor_tensor(
+            out=feat_stats[:, :, 2:3], in0=feat_sum[:].unsqueeze(2), in1=feat_stats[:, :, 1:2], op=ALU.mult
+        )
+        nc.vector.tensor_tensor(
+            out=feat_stats[:, :, 2:3], in0=feat_sq[:].unsqueeze(2), in1=feat_stats[:, :, 2:3], op=ALU.subtract
+        )
+        nc.vector.tensor_scalar(
+            out=feat_stats[:, :, 2:3], in0=feat_stats[:, :, 2:3], scalar1=K * LN_EPS, scalar2=None, op0=ALU.add
+        )
+
+        col = keep.tile([P, len(column_vectors), PACK], F32, name="col")
+        nc.vector.tensor_copy(out=col[:], in_=vec_bf[:, :, 0:PACK])
+
+        w_codes = []
+        w_scales = []
+        for kind in range(KINDS):
+            grouped_w = keep.tile([P, D_OUT, PACK], BF16, name="grouped_w%d" % kind, align_bytes=64)
+            nc.scalar.copy(
+                out=grouped_w[:].rearrange("p (c i) t -> p c t i", i=4),
+                in_=w_raw[kind][:].rearrange("p t (c i) -> p c t i", i=4),
+            )
+            codes = keep.tile([P, D_OUT], U32, name="w_codes%d" % kind, align_bytes=64)
+            scales = keep.tile([P, D_OUT], U8, name="w_scales%d" % kind, align_bytes=64)
+            nc.vector.quantize_mx(
+                out=codes[:].bitcast(FP8X4), scales=scales[:], in_=grouped_w[:].rearrange("p n t -> p (n t)")
+            )
+            w_codes.append(codes)
+            w_scales.append(scales)
+
+        def statistics(g):
+            x_sb = x_tiles[g]
+            mean_var = small.tile([P, GROUP, 2], F32, name="mean_var")
+            for i in range(GROUP):
+                nc.vector.bn_stats(out=stats[:, g * GROUP + i, 0:6], in_=x_sb[:, i, :])
+            for i in range(GROUP):
+                nc.vector.bn_aggr(out=mean_var[:, i, :], in_=stats[:, g * GROUP + i, :])
+            rstd = small.tile([P, GROUP, 1], F32, name="rstd")
+            nc.gpsimd.tensor_tensor(out=rstd[:], in0=mean_var[:, :, 1:2], in1=neg_half[:], op=ALU.pow)
+            return mean_var, rstd
+
+        def normalise(g):
+            x_sb = x_tiles[g]
+            mean_var, rstd = row_stats[g]
+            shift = small.tile([P, GROUP, 1], F32, name="shift")
+            nc.vector.scalar_tensor_tensor(
+                out=shift[:], in0=mean_var[:, :, 0:1], scalar=-1.0, in1=rstd[:], op0=ALU.mult, op1=ALU.mult
+            )
+            u = u_pool.tile([P, GROUP, PACK, P], F32, name="u")
+            raw = x_sb[:].rearrange("r i (p t) -> r i t p", t=PACK)
+            for i in range(GROUP):
+                if i < SCALAR_SHARE:
+                    nc.scalar.activation(
+                        out=u[:, i, :, 0:RAW_PARTS],
+                        in_=raw[:, i],
+                        func=ACT.Identity,
+                        scale=rstd[:, i, :],
+                        bias=shift[:, i, :],
+                    )
+                else:
+                    nc.gpsimd.tensor_scalar(
+                        out=u[:, i, :, 0:RAW_PARTS],
+                        in0=raw[:, i],
+                        scalar1=rstd[:, i, :],
+                        scalar2=shift[:, i, :],
+                        op0=ALU.mult,
+                        op1=ALU.add,
+                    )
+            centred = small.tile([P, GROUP, T2V], F32, name="centred")
+            nc.gpsimd.tensor_tensor(
+                out=centred[:],
+                in0=feat[:, :, g * GROUP : (g + 1) * GROUP].rearrange("p j g -> p g j"),
+                in1=mean_var[:, :, 0:1].to_broadcast([P, GROUP, T2V]),
+                op=ALU.subtract,
+            )
+            nc.gpsimd.tensor_tensor(
+                out=u[:, :, :, RAW_PARTS:P],
+                in0=centred[:].rearrange("r i (p t) -> r i t p", t=PACK),
+                in1=rstd[:].unsqueeze(3).to_broadcast([P, GROUP, PACK, T2V_PARTS]),
+                op=ALU.mult,
+            )
+            return u
+
+        def transpose_and_scale(g):
+            kind = g // GROUPS
+            u = u_tiles[g]
+            planes = q_pool.tile([P, PACK, GROUP * P], BF16, name="planes")
+            for t in range(PACK):
+                tp = psum_t.tile([P, GROUP * P], F32, name="tp")
+                for i in range(GROUP):
+                    nc.tensor.transpose(tp[:, i * P : (i + 1) * P], u[:, i, t, :], identity[:])
+                nc.scalar.activation(
+                    out=planes[:, t, :],
+                    in_=tp[:],
+                    func=ACT.Identity,
+                    scale=col[:, 2 * kind, t : t + 1],
+                    bias=col[:, 2 * kind + 1, t : t + 1],
+                )
+            return planes
+
+        def regroup(g):
+            planes = plane_tiles[g]
+            grouped = q_pool.tile([P, GROUP * P, PACK], BF16, name="grouped", align_bytes=64)
+            nc.vector.tensor_copy(
+                out=grouped[:].rearrange("p (c i) t -> p c t i", i=4),
+                in_=planes[:].rearrange("p t (c i) -> p c t i", i=4),
+            )
+            return grouped
+
+        def quantise(g):
+            grouped = grouped_tiles[g]
+            codes = q_pool.tile([P, GROUP * P], U32, name="codes", align_bytes=64)
+            scales = q_pool.tile([P, GROUP * P], U8, name="scales", align_bytes=64)
+            nc.vector.quantize_mx(
+                out=codes[:].bitcast(FP8X4), scales=scales[:], in_=grouped[:].rearrange("p r t -> p (r t)")
+            )
+            return codes, scales
+
+        def project_and_store(g, codes, scales):
+            kind, first = divmod(g, GROUPS)
+            first *= GROUP
+            o_sb = o_pool.tile([P, GROUP, D_OUT], F32, name="o_sb")
+            for pair in range(GROUP // 2):
+                acc = psum_o.tile([P, 2, D_OUT], F32, name="acc")
+                for i in range(2):
+                    rows = slice((2 * pair + i) * P, (2 * pair + i + 1) * P)
+                    nc.tensor.matmul_mx(
+                        out=acc[:, i, :],
+                        lhsT=codes[:, rows].bitcast(FP8X4),
+                        lhsT_scale=scales[:, rows],
+                        rhs=w_codes[kind][:].bitcast(FP8X4),
+                        rhs_scale=w_scales[kind][:],
+                        start=True,
+                        stop=True,
+                    )
+                nc.scalar.activation(out=o_sb[:, 2 * pair : 2 * pair + 2, :], in_=acc[:], func=ACT.Gelu)
+            out_rows = out[kind].rearrange("(p t) d -> p t d", t=TILES)
+            nc.sync.dma_start(out=out_rows[:, first : first + GROUP, :], in_=o_sb[:])
+
+        n_groups = KINDS * GROUPS
+        row_stats = {}
+        u_tiles = {}
+        plane_tiles = {}
+        grouped_tiles = {}
+        with tc.manual_schedule():
+            for n in range(-STATS_AHEAD, n_groups + 1):
+                if 0 <= n - 1:
+                    grouped_tiles[n - 1] = regroup(n - 1)
+                if 0 <= n < n_groups:
+                    plane_tiles[n] = transpose_and_scale(n)
+                if 0 <= n + NORM_AHEAD < n_groups:
+                    u_tiles[n + NORM_AHEAD] = normalise(n + NORM_AHEAD)
+                if 0 <= n - 1:
+                    codes, scales = quantise(n - 1)
+                    project_and_store(n - 1, codes, scales)
+                if LOAD_AHEAD - STATS_AHEAD <= n + LOAD_AHEAD < n_groups:
+                    x_tiles[n + LOAD_AHEAD] = load_group(n + LOAD_AHEAD)
+                if n + STATS_AHEAD < n_groups:
+                    row_stats[n + STATS_AHEAD] = statistics(n + STATS_AHEAD)

@@ -18,17 +18,23 @@ RAW = 500
 T2V = 12
 K = RAW + T2V
 PACK = 4
+RAW_PARTS = RAW // PACK
+T2V_PARTS = T2V // PACK
 D_OUT = 256
 KINDS = 2
 TILES = ROWS // P
+ALL_TILES = KINDS * TILES
 GROUP = 4
 GROUPS = TILES // GROUP
+N_GROUPS = KINDS * GROUPS
 LN_EPS = 1e-5
 ROUND_MAGIC = 12582912.0
-RAW_PARTS = RAW // PACK
-T2V_PARTS = T2V // PACK
-SCALAR_SHARE = 2
-LOAD_AHEAD = 6
+NORM_ENGINES = ("scalar", "vector", "gpsimd", "gpsimd")
+FIRST_NORM_ENGINES = ("scalar", "scalar", "gpsimd", "gpsimd")
+LAST_NORM_ENGINES = ("vector", "vector", "gpsimd", "gpsimd")
+LAST_BANKS_ON_VECTOR = 1
+EARLY_TILES = 32
+LOAD_AHEAD = 7
 STATS_AHEAD = 4
 NORM_AHEAD = 2
 
@@ -61,12 +67,13 @@ def tile_featureprojector_pa_t_kernel(
     with ExitStack() as ctx:
         keep = ctx.enter_context(tc.tile_pool(name="keep", bufs=1))
         x_pool = ctx.enter_context(tc.tile_pool(name="x_pool", bufs=LOAD_AHEAD - NORM_AHEAD + 2))
-        small = ctx.enter_context(tc.tile_pool(name="small", bufs=STATS_AHEAD - NORM_AHEAD + 2))
+        small = ctx.enter_context(tc.tile_pool(name="small", bufs=4))
         u_pool = ctx.enter_context(tc.tile_pool(name="u_pool", bufs=NORM_AHEAD + 2))
         q_pool = ctx.enter_context(tc.tile_pool(name="q_pool", bufs=3))
         o_pool = ctx.enter_context(tc.tile_pool(name="o_pool", bufs=3))
         psum_t = ctx.enter_context(tc.psum_pool(name="psum_t", bufs=6))
         psum_o = ctx.enter_context(tc.psum_pool(name="psum_o", bufs=2))
+        ctx.enter_context(tc.manual_schedule())
 
         ts_bf = keep.tile([P, KINDS, TILES], BF16, name="ts_bf")
         for kind in range(KINDS):
@@ -86,7 +93,7 @@ def tile_featureprojector_pa_t_kernel(
             nc.sync.dma_start(out=x_sb[:], in_=rows[:, first : first + GROUP, :])
             return x_sb
 
-        x_tiles = {0: load_group(0)}
+        x_tiles = {0: load_group(0), 1: load_group(1)}
 
         vec_bf = keep.tile([P, len(column_vectors), 16], BF16, name="vec_bf")
         for v in range(len(column_vectors)):
@@ -99,9 +106,11 @@ def tile_featureprojector_pa_t_kernel(
             raw = keep.tile([P, PACK, D_OUT], BF16, name="w_raw%d" % kind)
             nc.sync.dma_start(out=raw[:], in_=weights[kind].rearrange("(p t) n -> p t n", t=PACK))
             w_raw.append(raw)
-        for g in range(1, LOAD_AHEAD - STATS_AHEAD):
+        for g in range(2, LOAD_AHEAD - NORM_AHEAD):
             x_tiles[g] = load_group(g)
 
+        warm = keep.tile([P, 1], F32, name="warm")
+        nc.vector.memset(warm[:], 0.0)
         identity = keep.tile([P, P], F32, name="identity")
         make_identity(nc, identity[:])
         neg_half = keep.tile([P, GROUP, 1], F32, name="neg_half")
@@ -110,165 +119,185 @@ def tile_featureprojector_pa_t_kernel(
         slope = keep.tile([P, T2V], F32, name="slope")
         phase = keep.tile([P, T2V], F32, name="phase")
         turn = 1.0 / (2.0 * math.pi)
-        nc.vector.tensor_copy(out=slope[:, 0:1], in_=w0_bf[:])
-        nc.vector.tensor_copy(out=phase[:, 0:1], in_=b_bf[:, 0:1])
-        nc.vector.tensor_scalar(out=slope[:, 1:T2V], in0=w_bf[:], scalar1=turn, scalar2=None, op0=ALU.mult)
-        nc.vector.tensor_scalar(out=phase[:, 1:T2V], in0=b_bf[:, 1:T2V], scalar1=turn, scalar2=None, op0=ALU.mult)
-        all_tiles = KINDS * TILES
-        feat = keep.tile([P, T2V, all_tiles], F32, name="feat")
-        for j in range(T2V):
-            nc.scalar.activation(
-                out=feat[:, j, :],
-                in_=ts_bf[:].rearrange("p a t -> p (a t)"),
-                func=ACT.Identity,
-                scale=slope[:, j : j + 1],
-                bias=phase[:, j : j + 1],
-            )
-        sines = feat[:, 1:T2V, :]
-        whole = keep.tile([P, T2V - 1, all_tiles], F32, name="whole")
-        nc.vector.tensor_scalar(
-            out=whole[:], in0=sines, scalar1=ROUND_MAGIC, scalar2=ROUND_MAGIC, op0=ALU.add, op1=ALU.subtract
-        )
-        nc.vector.tensor_tensor(out=sines, in0=sines, in1=whole[:], op=ALU.subtract)
-        nc.scalar.activation(out=sines, in_=sines, func=ACT.Sin, scale=2.0 * math.pi)
-
-        squares = keep.tile([P, T2V, all_tiles], F32, name="squares")
-        nc.scalar.activation(out=squares[:], in_=feat[:], func=ACT.Square)
-        feat_sum = keep.tile([P, all_tiles], F32, name="feat_sum")
-        feat_sq = keep.tile([P, all_tiles], F32, name="feat_sq")
-        nc.vector.tensor_reduce(
-            out=feat_sum[:], in_=feat[:].rearrange("p j g -> p g j"), axis=mybir.AxisListType.X, op=ALU.add
-        )
-        nc.vector.tensor_reduce(
-            out=feat_sq[:], in_=squares[:].rearrange("p j g -> p g j"), axis=mybir.AxisListType.X, op=ALU.add
-        )
-        stats = keep.tile([P, all_tiles, 9], F32, name="stats")
+        feat = keep.tile([P, T2V, ALL_TILES], F32, name="feat")
+        whole = keep.tile([P, T2V - 1, ALL_TILES], F32, name="whole")
+        squares = keep.tile([P, T2V, ALL_TILES], F32, name="squares")
+        stats = keep.tile([P, ALL_TILES, 9], F32, name="stats")
         feat_stats = stats[:, :, 6:9]
+
+        nc.scalar.activation(out=warm[:], in_=warm[:], func=ACT.Sin)
         nc.vector.memset(feat_stats[:, :, 0:1], float(T2V))
-        nc.vector.tensor_scalar(
-            out=feat_stats[:, :, 1:2], in0=feat_sum[:].unsqueeze(2), scalar1=1.0 / T2V, scalar2=None, op0=ALU.mult
-        )
-        nc.vector.tensor_tensor(
-            out=feat_stats[:, :, 2:3], in0=feat_sum[:].unsqueeze(2), in1=feat_stats[:, :, 1:2], op=ALU.mult
-        )
-        nc.vector.tensor_tensor(
-            out=feat_stats[:, :, 2:3], in0=feat_sq[:].unsqueeze(2), in1=feat_stats[:, :, 2:3], op=ALU.subtract
-        )
-        nc.vector.tensor_scalar(
-            out=feat_stats[:, :, 2:3], in0=feat_stats[:, :, 2:3], scalar1=K * LN_EPS, scalar2=None, op0=ALU.add
-        )
+        nc.vector.tensor_copy(out=slope[:, 0:1], in_=w0_bf[:])
+        nc.vector.tensor_scalar(out=slope[:, 1:T2V], in0=w_bf[:], scalar1=turn, scalar2=None, op0=ALU.mult)
+        nc.vector.tensor_copy(out=phase[:, 0:1], in_=b_bf[:, 0:1])
+        nc.vector.tensor_scalar(out=phase[:, 1:T2V], in0=b_bf[:, 1:T2V], scalar1=turn, scalar2=None, op0=ALU.mult)
 
-        col = keep.tile([P, len(column_vectors), PACK], F32, name="col")
-        nc.vector.tensor_copy(out=col[:], in_=vec_bf[:, :, 0:PACK])
+        def t2v_arguments(part):
+            for j in range(T2V):
+                nc.scalar.activation(
+                    out=feat[:, j, part],
+                    in_=ts_bf[:].rearrange("p a t -> p (a t)")[:, part],
+                    func=ACT.Identity,
+                    scale=slope[:, j : j + 1],
+                    bias=phase[:, j : j + 1],
+                )
 
-        w_codes = []
-        w_scales = []
-        for kind in range(KINDS):
+        def t2v_fold(part):
+            sines = feat[:, 1:T2V, part]
+            nc.vector.tensor_scalar(
+                out=whole[:, :, part], in0=sines, scalar1=ROUND_MAGIC, scalar2=ROUND_MAGIC, op0=ALU.add, op1=ALU.subtract
+            )
+            nc.vector.tensor_tensor(out=sines, in0=sines, in1=whole[:, :, part], op=ALU.subtract)
+
+        def t2v_sines(part):
+            sines = feat[:, 1:T2V, part]
+            nc.scalar.activation(out=sines, in_=sines, func=ACT.Sin, scale=2.0 * math.pi)
+
+        def t2v_squares(part):
+            nc.scalar.activation(out=squares[:, :, part], in_=feat[:, :, part], func=ACT.Square)
+
+        def t2v_sum(source, part, half, steps):
+            for count, rest in steps:
+                terms = source[:, :, part] if count == T2V else half[:]
+                nc.gpsimd.tensor_tensor(
+                    out=half[:, 0:rest, :], in0=terms[:, 0:rest, :], in1=terms[:, rest : 2 * rest, :], op=ALU.add
+                )
+                if count % 2:
+                    nc.gpsimd.tensor_tensor(
+                        out=half[:, 0:1, :], in0=half[:, 0:1, :], in1=terms[:, count - 1 : count, :], op=ALU.add
+                    )
+
+        halvings = ((12, 6), (6, 3), (3, 1))
+
+        def new_half(name, part):
+            return keep.tile([P, T2V // 2, part.stop - part.start], F32, name=name)
+
+        def t2v_tuples(part, feat_half, sq_half):
+            tuples = feat_stats[:, part, :]
+            feat_sum = feat_half[:, 0, :].unsqueeze(2)
+            feat_sq = sq_half[:, 0, :].unsqueeze(2)
+            nc.vector.tensor_scalar(
+                out=tuples[:, :, 1:2], in0=feat_sum, scalar1=1.0 / T2V, scalar2=None, op0=ALU.mult
+            )
+            nc.vector.tensor_tensor(out=tuples[:, :, 2:3], in0=feat_sum, in1=tuples[:, :, 1:2], op=ALU.mult)
+            nc.vector.tensor_tensor(out=tuples[:, :, 2:3], in0=feat_sq, in1=tuples[:, :, 2:3], op=ALU.subtract)
+            nc.vector.tensor_scalar(
+                out=tuples[:, :, 2:3], in0=tuples[:, :, 2:3], scalar1=K * LN_EPS, scalar2=None, op0=ALU.add
+            )
+
+        def regroup_weights(kind):
             grouped_w = keep.tile([P, D_OUT, PACK], BF16, name="grouped_w%d" % kind, align_bytes=64)
             nc.scalar.copy(
                 out=grouped_w[:].rearrange("p (c i) t -> p c t i", i=4),
                 in_=w_raw[kind][:].rearrange("p t (c i) -> p c t i", i=4),
             )
+            return grouped_w
+
+        def quantise_weights(kind, grouped_w):
             codes = keep.tile([P, D_OUT], U32, name="w_codes%d" % kind, align_bytes=64)
             scales = keep.tile([P, D_OUT], U8, name="w_scales%d" % kind, align_bytes=64)
             nc.vector.quantize_mx(
                 out=codes[:].bitcast(FP8X4), scales=scales[:], in_=grouped_w[:].rearrange("p n t -> p (n t)")
             )
-            w_codes.append(codes)
-            w_scales.append(scales)
+            return codes, scales
 
-        def statistics(g):
-            x_sb = x_tiles[g]
+        def statistics(g, tiles):
+            for i in tiles:
+                nc.vector.bn_stats(out=stats[:, g * GROUP + i, 0:6], in_=x_tiles[g][:, i, :])
+
+        def aggregate(g):
             mean_var = small.tile([P, GROUP, 2], F32, name="mean_var")
-            for i in range(GROUP):
-                nc.vector.bn_stats(out=stats[:, g * GROUP + i, 0:6], in_=x_sb[:, i, :])
             for i in range(GROUP):
                 nc.vector.bn_aggr(out=mean_var[:, i, :], in_=stats[:, g * GROUP + i, :])
             rstd = small.tile([P, GROUP, 1], F32, name="rstd")
             nc.gpsimd.tensor_tensor(out=rstd[:], in0=mean_var[:, :, 1:2], in1=neg_half[:], op=ALU.pow)
             return mean_var, rstd
 
-        def normalise(g):
-            x_sb = x_tiles[g]
+        def shift_of(g):
             mean_var, rstd = row_stats[g]
             shift = small.tile([P, GROUP, 1], F32, name="shift")
             nc.vector.scalar_tensor_tensor(
                 out=shift[:], in0=mean_var[:, :, 0:1], scalar=-1.0, in1=rstd[:], op0=ALU.mult, op1=ALU.mult
             )
-            u = u_pool.tile([P, GROUP, PACK, P], F32, name="u")
-            raw = x_sb[:].rearrange("r i (p t) -> r i t p", t=PACK)
-            for i in range(GROUP):
-                if i < SCALAR_SHARE:
-                    nc.scalar.activation(
-                        out=u[:, i, :, 0:RAW_PARTS],
-                        in_=raw[:, i],
-                        func=ACT.Identity,
-                        scale=rstd[:, i, :],
-                        bias=shift[:, i, :],
-                    )
-                else:
-                    nc.gpsimd.tensor_scalar(
-                        out=u[:, i, :, 0:RAW_PARTS],
-                        in0=raw[:, i],
-                        scalar1=rstd[:, i, :],
-                        scalar2=shift[:, i, :],
-                        op0=ALU.mult,
-                        op1=ALU.add,
-                    )
-            centred = small.tile([P, GROUP, T2V], F32, name="centred")
-            nc.gpsimd.tensor_tensor(
-                out=centred[:],
-                in0=feat[:, :, g * GROUP : (g + 1) * GROUP].rearrange("p j g -> p g j"),
-                in1=mean_var[:, :, 0:1].to_broadcast([P, GROUP, T2V]),
-                op=ALU.subtract,
-            )
-            nc.gpsimd.tensor_tensor(
-                out=u[:, :, :, RAW_PARTS:P],
-                in0=centred[:].rearrange("r i (p t) -> r i t p", t=PACK),
-                in1=rstd[:].unsqueeze(3).to_broadcast([P, GROUP, PACK, T2V_PARTS]),
-                op=ALU.mult,
-            )
-            return u
+            return shift
 
-        def transpose_and_scale(g):
-            kind = g // GROUPS
-            u = u_tiles[g]
-            planes = q_pool.tile([P, PACK, GROUP * P], BF16, name="planes")
+        def norm_engines(g):
+            if g < NORM_AHEAD:
+                return FIRST_NORM_ENGINES
+            return NORM_ENGINES if g - NORM_AHEAD + STATS_AHEAD < N_GROUPS else LAST_NORM_ENGINES
+
+        def new_u():
+            return u_pool.tile([P, GROUP, PACK, P], F32, name="u")
+
+        def normalise(g, engine):
+            rstd = row_stats[g][1]
+            shift = shift_tiles[g]
+            for i in range(GROUP):
+                if norm_engines(g)[i] != engine:
+                    continue
+                sources = (x_tiles[g][:, i, :], feat[:, :, g * GROUP + i])
+                places = (slice(0, RAW_PARTS), slice(RAW_PARTS, P))
+                for source, place in zip(sources, places):
+                    source = source.rearrange("r (p t) -> r t p", t=PACK)
+                    result = u_tiles[g][:, i, :, place]
+                    if engine == "scalar":
+                        nc.scalar.activation(
+                            out=result, in_=source, func=ACT.Identity, scale=rstd[:, i, :], bias=shift[:, i, :]
+                        )
+                    else:
+                        (nc.vector if engine == "vector" else nc.gpsimd).tensor_scalar(
+                            out=result,
+                            in0=source,
+                            scalar1=rstd[:, i, :],
+                            scalar2=shift[:, i, :],
+                            op0=ALU.mult,
+                            op1=ALU.add,
+                        )
+
+        def transpose(g):
+            banks = []
             for t in range(PACK):
                 tp = psum_t.tile([P, GROUP * P], F32, name="tp")
                 for i in range(GROUP):
-                    nc.tensor.transpose(tp[:, i * P : (i + 1) * P], u[:, i, t, :], identity[:])
-                nc.scalar.activation(
-                    out=planes[:, t, :],
-                    in_=tp[:],
-                    func=ACT.Identity,
-                    scale=col[:, 2 * kind, t : t + 1],
-                    bias=col[:, 2 * kind + 1, t : t + 1],
-                )
-            return planes
+                    nc.tensor.transpose(tp[:, i * P : (i + 1) * P], u_tiles[g][:, i, t, :], identity[:])
+                banks.append(tp)
+            return banks
+
+        def scale(g, engine):
+            kind = g // GROUPS
+            on_vector = LAST_BANKS_ON_VECTOR if g + STATS_AHEAD >= N_GROUPS else 0
+            for t in range(PACK):
+                gamma = col[:, 2 * kind, t : t + 1]
+                beta = col[:, 2 * kind + 1, t : t + 1]
+                result = plane_tiles[g][:, t, :]
+                if engine == "scalar" and t < PACK - on_vector:
+                    nc.scalar.activation(out=result, in_=bank_tiles[g][t][:], func=ACT.Identity, scale=gamma, bias=beta)
+                if engine == "vector" and t >= PACK - on_vector:
+                    nc.vector.tensor_scalar(
+                        out=result, in0=bank_tiles[g][t][:], scalar1=gamma, scalar2=beta, op0=ALU.mult, op1=ALU.add
+                    )
 
         def regroup(g):
-            planes = plane_tiles[g]
             grouped = q_pool.tile([P, GROUP * P, PACK], BF16, name="grouped", align_bytes=64)
             nc.vector.tensor_copy(
                 out=grouped[:].rearrange("p (c i) t -> p c t i", i=4),
-                in_=planes[:].rearrange("p t (c i) -> p c t i", i=4),
+                in_=plane_tiles[g][:].rearrange("p t (c i) -> p c t i", i=4),
             )
             return grouped
 
         def quantise(g):
-            grouped = grouped_tiles[g]
             codes = q_pool.tile([P, GROUP * P], U32, name="codes", align_bytes=64)
             scales = q_pool.tile([P, GROUP * P], U8, name="scales", align_bytes=64)
             nc.vector.quantize_mx(
-                out=codes[:].bitcast(FP8X4), scales=scales[:], in_=grouped[:].rearrange("p r t -> p (r t)")
+                out=codes[:].bitcast(FP8X4), scales=scales[:], in_=grouped_tiles[g][:].rearrange("p r t -> p (r t)")
             )
             return codes, scales
 
-        def project_and_store(g, codes, scales):
-            kind, first = divmod(g, GROUPS)
-            first *= GROUP
-            o_sb = o_pool.tile([P, GROUP, D_OUT], F32, name="o_sb")
+        def project(g):
+            kind = g // GROUPS
+            codes, scales = quantised[g]
+            w_codes, w_scales = w_quantised[kind]
+            accs = []
             for pair in range(GROUP // 2):
                 acc = psum_o.tile([P, 2, D_OUT], F32, name="acc")
                 for i in range(2):
@@ -277,32 +306,100 @@ def tile_featureprojector_pa_t_kernel(
                         out=acc[:, i, :],
                         lhsT=codes[:, rows].bitcast(FP8X4),
                         lhsT_scale=scales[:, rows],
-                        rhs=w_codes[kind][:].bitcast(FP8X4),
-                        rhs_scale=w_scales[kind][:],
+                        rhs=w_codes[:].bitcast(FP8X4),
+                        rhs_scale=w_scales[:],
                         start=True,
                         stop=True,
                     )
-                nc.scalar.activation(out=o_sb[:, 2 * pair : 2 * pair + 2, :], in_=acc[:], func=ACT.Gelu)
+                accs.append(acc)
+            return accs
+
+        def gelu_and_store(g):
+            kind, first = divmod(g, GROUPS)
+            first *= GROUP
+            o_sb = o_pool.tile([P, GROUP, D_OUT], F32, name="o_sb")
+            for pair in range(GROUP // 2):
+                nc.scalar.activation(out=o_sb[:, 2 * pair : 2 * pair + 2, :], in_=acc_tiles[g][pair][:], func=ACT.Gelu)
             out_rows = out[kind].rearrange("(p t) d -> p t d", t=TILES)
             nc.sync.dma_start(out=out_rows[:, first : first + GROUP, :], in_=o_sb[:])
 
-        n_groups = KINDS * GROUPS
         row_stats = {}
+        shift_tiles = {}
         u_tiles = {}
+        bank_tiles = {}
         plane_tiles = {}
         grouped_tiles = {}
-        with tc.manual_schedule():
-            for n in range(-STATS_AHEAD, n_groups + 1):
-                if 0 <= n - 1:
-                    grouped_tiles[n - 1] = regroup(n - 1)
-                if 0 <= n < n_groups:
-                    plane_tiles[n] = transpose_and_scale(n)
-                if 0 <= n + NORM_AHEAD < n_groups:
-                    u_tiles[n + NORM_AHEAD] = normalise(n + NORM_AHEAD)
-                if 0 <= n - 1:
-                    codes, scales = quantise(n - 1)
-                    project_and_store(n - 1, codes, scales)
-                if LOAD_AHEAD - STATS_AHEAD <= n + LOAD_AHEAD < n_groups:
-                    x_tiles[n + LOAD_AHEAD] = load_group(n + LOAD_AHEAD)
-                if n + STATS_AHEAD < n_groups:
-                    row_stats[n + STATS_AHEAD] = statistics(n + STATS_AHEAD)
+        quantised = {}
+        acc_tiles = {}
+
+        def round_of(n):
+            last, this, ahead, new = n - 1, n, n + NORM_AHEAD, n + STATS_AHEAD
+            if 0 < ahead < N_GROUPS:
+                shift_tiles[ahead] = shift_of(ahead)
+            if 0 <= last:
+                grouped_tiles[last] = regroup(last)
+            if 0 <= this < N_GROUPS:
+                plane_tiles[this] = q_pool.tile([P, PACK, GROUP * P], BF16, name="planes")
+                scale(this, "scalar")
+            if new < N_GROUPS:
+                statistics(new, range(1))
+            if 0 <= last:
+                quantised[last] = quantise(last)
+                acc_tiles[last] = project(last)
+            if ahead < N_GROUPS:
+                u_tiles[ahead] = new_u()
+                normalise(ahead, "vector")
+                normalise(ahead, "gpsimd")
+                normalise(ahead, "scalar")
+            if 0 <= this < N_GROUPS:
+                scale(this, "vector")
+            if 0 <= this + 1 < N_GROUPS:
+                bank_tiles[this + 1] = transpose(this + 1)
+            if 0 <= last:
+                gelu_and_store(last)
+            if new < N_GROUPS:
+                statistics(new, range(1, GROUP))
+                row_stats[new] = aggregate(new)
+            if n + LOAD_AHEAD < N_GROUPS:
+                x_tiles[n + LOAD_AHEAD] = load_group(n + LOAD_AHEAD)
+
+        early = slice(0, EARLY_TILES)
+        late = slice(EARLY_TILES, ALL_TILES)
+        early_halves = new_half("early_feat", early), new_half("early_sq", early)
+        late_halves = new_half("late_feat", late), new_half("late_sq", late)
+        t2v_arguments(early)
+        t2v_fold(early)
+        t2v_sines(early)
+        t2v_squares(early)
+        t2v_sum(feat, early, early_halves[0], halvings)
+        t2v_sum(squares, early, early_halves[1], halvings)
+        statistics(0, range(GROUP))
+        t2v_arguments(late)
+        t2v_fold(late)
+        t2v_tuples(early, *early_halves)
+        row_stats[0] = aggregate(0)
+        grouped_w = [regroup_weights(kind) for kind in range(KINDS)]
+        t2v_sines(late)
+        statistics(1, range(GROUP - 1))
+        shift_tiles[0] = shift_of(0)
+        statistics(1, range(GROUP - 1, GROUP))
+        row_stats[1] = aggregate(1)
+
+        round_of(-2)
+        t2v_squares(late)
+        col = keep.tile([P, len(column_vectors), PACK], F32, name="col")
+        nc.vector.tensor_copy(out=col[:], in_=vec_bf[:, :, 0:PACK])
+        round_of(-1)
+        w_quantised = [quantise_weights(kind, grouped_w[kind]) for kind in range(KINDS)]
+        late_pieces = [
+            (source, half, steps)
+            for steps in (halvings[:1], halvings[1:])
+            for source, half in zip((feat, squares), late_halves)
+        ]
+        for n in range(N_GROUPS + 1):
+            if n == len(late_pieces):
+                t2v_tuples(late, *late_halves)
+            round_of(n)
+            if n < len(late_pieces):
+                source, half, steps = late_pieces[n]
+                t2v_sum(source, late, half, steps)

@@ -29,9 +29,9 @@ GROUPS = TILES // GROUP
 N_GROUPS = KINDS * GROUPS
 LN_EPS = 1e-5
 ROUND_MAGIC = 12582912.0
-NORM_ENGINES = ("scalar", "vector", "gpsimd", "gpsimd")
+NORM_ENGINES = ("scalar", "scalar", "vector", "gpsimd")
 FIRST_NORM_ENGINES = ("scalar", "scalar", "gpsimd", "gpsimd")
-LAST_NORM_ENGINES = ("vector", "vector", "gpsimd", "gpsimd")
+LAST_NORM_ENGINES = ("scalar", "vector", "vector", "vector")
 LAST_BANKS_ON_VECTOR = 1
 EARLY_TILES = 32
 LOAD_AHEAD = 7
@@ -113,8 +113,6 @@ def tile_featureprojector_pa_t_kernel(
         nc.vector.memset(warm[:], 0.0)
         identity = keep.tile([P, P], F32, name="identity")
         make_identity(nc, identity[:])
-        neg_half = keep.tile([P, GROUP, 1], F32, name="neg_half")
-        nc.gpsimd.memset(neg_half[:], -0.5)
 
         slope = keep.tile([P, T2V], F32, name="slope")
         phase = keep.tile([P, T2V], F32, name="phase")
@@ -124,6 +122,11 @@ def tile_featureprojector_pa_t_kernel(
         squares = keep.tile([P, T2V, ALL_TILES], F32, name="squares")
         stats = keep.tile([P, ALL_TILES, 9], F32, name="stats")
         feat_stats = stats[:, :, 6:9]
+        mean_var = keep.tile([P, ALL_TILES, 2], F32, name="mean_var")
+        rstd = keep.tile([P, ALL_TILES, 1], F32, name="rstd")
+        shift = keep.tile([P, ALL_TILES, 1], F32, name="shift")
+        neg_half = keep.tile([P, GROUP, 1], F32, name="neg_half")
+        nc.gpsimd.memset(neg_half[:], -0.5)
 
         nc.scalar.activation(out=warm[:], in_=warm[:], func=ACT.Sin)
         nc.vector.memset(feat_stats[:, :, 0:1], float(T2V))
@@ -201,55 +204,60 @@ def tile_featureprojector_pa_t_kernel(
             )
             return codes, scales
 
-        def statistics(g, tiles):
-            for i in tiles:
+        def statistics(g):
+            for i in range(GROUP):
                 nc.vector.bn_stats(out=stats[:, g * GROUP + i, 0:6], in_=x_tiles[g][:, i, :])
 
         def aggregate(g):
-            mean_var = small.tile([P, GROUP, 2], F32, name="mean_var")
-            for i in range(GROUP):
-                nc.vector.bn_aggr(out=mean_var[:, i, :], in_=stats[:, g * GROUP + i, :])
-            rstd = small.tile([P, GROUP, 1], F32, name="rstd")
-            nc.gpsimd.tensor_tensor(out=rstd[:], in0=mean_var[:, :, 1:2], in1=neg_half[:], op=ALU.pow)
-            return mean_var, rstd
+            for i in range(g * GROUP, (g + 1) * GROUP):
+                nc.vector.bn_aggr(out=mean_var[:, i, :], in_=stats[:, i, :])
 
-        def shift_of(g):
-            mean_var, rstd = row_stats[g]
-            shift = small.tile([P, GROUP, 1], F32, name="shift")
+        def inverse_roots(g):
+            tiles = slice(g * GROUP, (g + 1) * GROUP)
+            nc.gpsimd.tensor_tensor(out=rstd[:, tiles, :], in0=mean_var[:, tiles, 1:2], in1=neg_half[:], op=ALU.pow)
+
+        def shifts(g):
+            tiles = slice(g * GROUP, (g + 1) * GROUP)
             nc.vector.scalar_tensor_tensor(
-                out=shift[:], in0=mean_var[:, :, 0:1], scalar=-1.0, in1=rstd[:], op0=ALU.mult, op1=ALU.mult
+                out=shift[:, tiles, :],
+                in0=mean_var[:, tiles, 0:1],
+                scalar=-1.0,
+                in1=rstd[:, tiles, :],
+                op0=ALU.mult,
+                op1=ALU.mult,
             )
-            return shift
 
         def norm_engines(g):
             if g < NORM_AHEAD:
                 return FIRST_NORM_ENGINES
-            return NORM_ENGINES if g - NORM_AHEAD + STATS_AHEAD < N_GROUPS else LAST_NORM_ENGINES
+            return NORM_ENGINES if g + STATS_AHEAD < N_GROUPS + NORM_AHEAD else LAST_NORM_ENGINES
 
         def new_u():
             return u_pool.tile([P, GROUP, PACK, P], F32, name="u")
 
         def normalise(g, engine):
-            rstd = row_stats[g][1]
-            shift = shift_tiles[g]
             for i in range(GROUP):
-                if norm_engines(g)[i] != engine:
-                    continue
-                sources = (x_tiles[g][:, i, :], feat[:, :, g * GROUP + i])
-                places = (slice(0, RAW_PARTS), slice(RAW_PARTS, P))
-                for source, place in zip(sources, places):
+                at = g * GROUP + i
+                owner = norm_engines(g)[i]
+                parts = (
+                    (owner, x_tiles[g][:, i, :], slice(0, RAW_PARTS)),
+                    ("scalar" if owner == "gpsimd" else owner, feat[:, :, at], slice(RAW_PARTS, P)),
+                )
+                for worker, source, place in parts:
+                    if worker != engine:
+                        continue
                     source = source.rearrange("r (p t) -> r t p", t=PACK)
                     result = u_tiles[g][:, i, :, place]
                     if engine == "scalar":
                         nc.scalar.activation(
-                            out=result, in_=source, func=ACT.Identity, scale=rstd[:, i, :], bias=shift[:, i, :]
+                            out=result, in_=source, func=ACT.Identity, scale=rstd[:, at, :], bias=shift[:, at, :]
                         )
                     else:
                         (nc.vector if engine == "vector" else nc.gpsimd).tensor_scalar(
                             out=result,
                             in0=source,
-                            scalar1=rstd[:, i, :],
-                            scalar2=shift[:, i, :],
+                            scalar1=rstd[:, at, :],
+                            scalar2=shift[:, at, :],
                             op0=ALU.mult,
                             op1=ALU.add,
                         )
@@ -323,8 +331,6 @@ def tile_featureprojector_pa_t_kernel(
             out_rows = out[kind].rearrange("(p t) d -> p t d", t=TILES)
             nc.sync.dma_start(out=out_rows[:, first : first + GROUP, :], in_=o_sb[:])
 
-        row_stats = {}
-        shift_tiles = {}
         u_tiles = {}
         bank_tiles = {}
         plane_tiles = {}
@@ -334,21 +340,23 @@ def tile_featureprojector_pa_t_kernel(
 
         def round_of(n):
             last, this, ahead, new = n - 1, n, n + NORM_AHEAD, n + STATS_AHEAD
-            if 0 < ahead < N_GROUPS:
-                shift_tiles[ahead] = shift_of(ahead)
+            if ahead < N_GROUPS:
+                shifts(ahead)
             if 0 <= last:
                 grouped_tiles[last] = regroup(last)
             if 0 <= this < N_GROUPS:
                 plane_tiles[this] = q_pool.tile([P, PACK, GROUP * P], BF16, name="planes")
                 scale(this, "scalar")
-            if new < N_GROUPS:
-                statistics(new, range(1))
-            if 0 <= last:
-                quantised[last] = quantise(last)
-                acc_tiles[last] = project(last)
             if ahead < N_GROUPS:
                 u_tiles[ahead] = new_u()
                 normalise(ahead, "vector")
+            if 0 <= last:
+                quantised[last] = quantise(last)
+                acc_tiles[last] = project(last)
+            if new - 1 < N_GROUPS:
+                aggregate(new - 1)
+                inverse_roots(new - 1)
+            if ahead < N_GROUPS:
                 normalise(ahead, "gpsimd")
                 normalise(ahead, "scalar")
             if 0 <= this < N_GROUPS:
@@ -358,8 +366,7 @@ def tile_featureprojector_pa_t_kernel(
             if 0 <= last:
                 gelu_and_store(last)
             if new < N_GROUPS:
-                statistics(new, range(1, GROUP))
-                row_stats[new] = aggregate(new)
+                statistics(new)
             if n + LOAD_AHEAD < N_GROUPS:
                 x_tiles[n + LOAD_AHEAD] = load_group(n + LOAD_AHEAD)
 
@@ -373,17 +380,15 @@ def tile_featureprojector_pa_t_kernel(
         t2v_squares(early)
         t2v_sum(feat, early, early_halves[0], halvings)
         t2v_sum(squares, early, early_halves[1], halvings)
-        statistics(0, range(GROUP))
+        statistics(0)
         t2v_arguments(late)
         t2v_fold(late)
         t2v_tuples(early, *early_halves)
-        row_stats[0] = aggregate(0)
+        aggregate(0)
+        inverse_roots(0)
         grouped_w = [regroup_weights(kind) for kind in range(KINDS)]
         t2v_sines(late)
-        statistics(1, range(GROUP - 1))
-        shift_tiles[0] = shift_of(0)
-        statistics(1, range(GROUP - 1, GROUP))
-        row_stats[1] = aggregate(1)
+        statistics(1)
 
         round_of(-2)
         t2v_squares(late)

import math
from contextlib import ExitStack

import concourse.mybir as mybir
from concourse.masks import make_identity

F32 = mybir.dt.float32
BF16 = mybir.dt.bfloat16
U32 = mybir.dt.uint32
U8 = mybir.dt.uint8
FP8X4 = mybir.dt.float8_e4m3fn_x4
ALU = mybir.AluOpType
ACT = mybir.ActivationFunctionType

P = 128
ROWS = 8192
RAW = 500
T2V = 12
K = RAW + T2V
PACK = 4
RAW_PARTS = RAW // PACK
T2V_PARTS = T2V // PACK
D_OUT = 256
KINDS = 2
TILES = ROWS // P
ALL_TILES = KINDS * TILES
GROUP = 4
GROUPS = TILES // GROUP
N_GROUPS = KINDS * GROUPS
LN_EPS = 1e-5
ROUND_MAGIC = 12582912.0
NORM_ENGINES = ("scalar", "scalar", "vector", "gpsimd")
FIRST_NORM_ENGINES = ("scalar", "scalar", "gpsimd", "gpsimd")
LAST_NORM_ENGINES = ("scalar", "vector", "vector", "vector")
LAST_BANKS_ON_VECTOR = 1
EARLY_TILES = 32
LOAD_AHEAD = 7
STATS_AHEAD = 4
NORM_AHEAD = 2

FLOPS = 2 * KINDS * ROWS * K * D_OUT


def tile_featureprojector_pa_t_kernel(
    tc,
    x_bill,
    ts_bill,
    x_bill_version,
    ts_bill_version,
    w0,
    w,
    b,
    gamma_bill,
    beta_bill,
    W_bill,
    gamma_bill_version,
    beta_bill_version,
    W_bill_version,
    out,
):
    nc = tc.nc
    xs = [x_bill, x_bill_version]
    stamps = [ts_bill, ts_bill_version]
    weights = [W_bill, W_bill_version]
    column_vectors = [gamma_bill, beta_bill, gamma_bill_version, beta_bill_version]

    with ExitStack() as ctx:
        keep = ctx.enter_context(tc.tile_pool(name="keep", bufs=1))
        x_pool = ctx.enter_context(tc.tile_pool(name="x_pool", bufs=LOAD_AHEAD - NORM_AHEAD + 2))
        small = ctx.enter_context(tc.tile_pool(name="small", bufs=4))
        u_pool = ctx.enter_context(tc.tile_pool(name="u_pool", bufs=NORM_AHEAD + 2))
        q_pool = ctx.enter_context(tc.tile_pool(name="q_pool", bufs=3))
        o_pool = ctx.enter_context(tc.tile_pool(name="o_pool", bufs=3))
        psum_t = ctx.enter_context(tc.psum_pool(name="psum_t", bufs=6))
        psum_o = ctx.enter_context(tc.psum_pool(name="psum_o", bufs=2))
        ctx.enter_context(tc.manual_schedule())

        ts_bf = keep.tile([P, KINDS, TILES], BF16, name="ts_bf")
        for kind in range(KINDS):
            nc.sync.dma_start(out=ts_bf[:, kind, :], in_=stamps[kind].rearrange("(p t) -> p t", t=TILES))
        w0_bf = keep.tile([P, 1], BF16, name="w0_bf")
        w_bf = keep.tile([P, T2V - 1], BF16, name="w_bf")
        b_bf = keep.tile([P, T2V], BF16, name="b_bf")
        nc.sync.dma_start(out=w0_bf[:], in_=w0.partition_broadcast(P))
        nc.sync.dma_start(out=w_bf[:], in_=w.partition_broadcast(P))
        nc.sync.dma_start(out=b_bf[:], in_=b.partition_broadcast(P))

        def load_group(g):
            kind, first = divmod(g, GROUPS)
            first *= GROUP
            x_sb = x_pool.tile([P, GROUP, RAW], BF16, name="x_sb")
            rows = xs[kind].rearrange("(p t) k -> p t k", t=TILES)
            nc.sync.dma_start(out=x_sb[:], in_=rows[:, first : first + GROUP, :])
            return x_sb

        x_tiles = {0: load_group(0), 1: load_group(1)}

        vec_bf = keep.tile([P, len(column_vectors), 16], BF16, name="vec_bf")
        for v in range(len(column_vectors)):
            nc.sync.dma_start(
                out=vec_bf[:, v, 0:PACK],
                in_=column_vectors[v].rearrange("(p t) -> p t", t=PACK),
            )
        w_raw = []
        for kind in range(KINDS):
            raw = keep.tile([P, PACK, D_OUT], BF16, name="w_raw%d" % kind)
            nc.sync.dma_start(out=raw[:], in_=weights[kind].rearrange("(p t) n -> p t n", t=PACK))
            w_raw.append(raw)
        for g in range(2, LOAD_AHEAD - NORM_AHEAD):
            x_tiles[g] = load_group(g)

        warm = keep.tile([P, 1], F32, name="warm")
        nc.vector.memset(warm[:], 0.0)
        identity = keep.tile([P, P], F32, name="identity")
        make_identity(nc, identity[:])

        slope = keep.tile([P, T2V], F32, name="slope")
        phase = keep.tile([P, T2V], F32, name="phase")
        turn = 1.0 / (2.0 * math.pi)
        feat = keep.tile([P, T2V, ALL_TILES], F32, name="feat")
        whole = keep.tile([P, T2V - 1, ALL_TILES], F32, name="whole")
        squares = keep.tile([P, T2V, ALL_TILES], F32, name="squares")
        stats = keep.tile([P, ALL_TILES, 9], F32, name="stats")
        feat_stats = stats[:, :, 6:9]
        mean_var = keep.tile([P, ALL_TILES, 2], F32, name="mean_var")
        rstd = keep.tile([P, ALL_TILES, 1], F32, name="rstd")
        shift = keep.tile([P, ALL_TILES, 1], F32, name="shift")
        neg_half = keep.tile([P, GROUP, 1], F32, name="neg_half")
        nc.gpsimd.memset(neg_half[:], -0.5)

        nc.scalar.activation(out=warm[:], in_=warm[:], func=ACT.Sin)
        nc.vector.memset(feat_stats[:, :, 0:1], float(T2V))
        nc.vector.tensor_copy(out=slope[:, 0:1], in_=w0_bf[:])
        nc.vector.tensor_scalar(out=slope[:, 1:T2V], in0=w_bf[:], scalar1=turn, scalar2=None, op0=ALU.mult)
        nc.vector.tensor_copy(out=phase[:, 0:1], in_=b_bf[:, 0:1])
        nc.vector.tensor_scalar(out=phase[:, 1:T2V], in0=b_bf[:, 1:T2V], scalar1=turn, scalar2=None, op0=ALU.mult)

        def t2v_arguments(part):
            for j in range(T2V):
                nc.scalar.activation(
                    out=feat[:, j, part],
                    in_=ts_bf[:].rearrange("p a t -> p (a t)")[:, part],
                    func=ACT.Identity,
                    scale=slope[:, j : j + 1],
                    bias=phase[:, j : j + 1],
                )

        def t2v_fold(part):
            sines = feat[:, 1:T2V, part]
            nc.vector.tensor_scalar(
                out=whole[:, :, part], in0=sines, scalar1=ROUND_MAGIC, scalar2=ROUND_MAGIC, op0=ALU.add, op1=ALU.subtract
            )
            nc.vector.tensor_tensor(out=sines, in0=sines, in1=whole[:, :, part], op=ALU.subtract)

        def t2v_sines(part):
            sines = feat[:, 1:T2V, part]
            nc.scalar.activation(out=sines, in_=sines, func=ACT.Sin, scale=2.0 * math.pi)

        def t2v_squares(part):
            nc.scalar.activation(out=squares[:, :, part], in_=feat[:, :, part], func=ACT.Square)

        def t2v_sum(source, part, half, steps):
            for count, rest in steps:
                terms = source[:, :, part] if count == T2V else half[:]
                nc.gpsimd.tensor_tensor(
                    out=half[:, 0:rest, :], in0=terms[:, 0:rest, :], in1=terms[:, rest : 2 * rest, :], op=ALU.add
                )
                if count % 2:
                    nc.gpsimd.tensor_tensor(
                        out=half[:, 0:1, :], in0=half[:, 0:1, :], in1=terms[:, count - 1 : count, :], op=ALU.add
                    )

        halvings = ((12, 6), (6, 3), (3, 1))

        def new_half(name, part):
            return keep.tile([P, T2V // 2, part.stop - part.start], F32, name=name)

        def t2v_tuples(part, feat_half, sq_half):
            tuples = feat_stats[:, part, :]
            feat_sum = feat_half[:, 0, :].unsqueeze(2)
            feat_sq = sq_half[:, 0, :].unsqueeze(2)
            nc.vector.tensor_scalar(
                out=tuples[:, :, 1:2], in0=feat_sum, scalar1=1.0 / T2V, scalar2=None, op0=ALU.mult
            )
            nc.vector.tensor_tensor(out=tuples[:, :, 2:3], in0=feat_sum, in1=tuples[:, :, 1:2], op=ALU.mult)
            nc.vector.tensor_tensor(out=tuples[:, :, 2:3], in0=feat_sq, in1=tuples[:, :, 2:3], op=ALU.subtract)
            nc.vector.tensor_scalar(
                out=tuples[:, :, 2:3], in0=tuples[:, :, 2:3], scalar1=K * LN_EPS, scalar2=None, op0=ALU.add
            )

        def regroup_weights(kind):
            grouped_w = keep.tile([P, D_OUT, PACK], BF16, name="grouped_w%d" % kind, align_bytes=64)
            nc.scalar.copy(
                out=grouped_w[:].rearrange("p (c i) t -> p c t i", i=4),
                in_=w_raw[kind][:].rearrange("p t (c i) -> p c t i", i=4),
            )
            return grouped_w

        def quantise_weights(kind, grouped_w):
            codes = keep.tile([P, D_OUT], U32, name="w_codes%d" % kind, align_bytes=64)
            scales = keep.tile([P, D_OUT], U8, name="w_scales%d" % kind, align_bytes=64)
            nc.vector.quantize_mx(
                out=codes[:].bitcast(FP8X4), scales=scales[:], in_=grouped_w[:].rearrange("p n t -> p (n t)")
            )
            return codes, scales

        def statistics(g):
            for i in range(GROUP):
                nc.vector.bn_stats(out=stats[:, g * GROUP + i, 0:6], in_=x_tiles[g][:, i, :])

        def aggregate(g):
            for i in range(g * GROUP, (g + 1) * GROUP):
                nc.vector.bn_aggr(out=mean_var[:, i, :], in_=stats[:, i, :])

        def inverse_roots(g):
            tiles = slice(g * GROUP, (g + 1) * GROUP)
            nc.gpsimd.tensor_tensor(out=rstd[:, tiles, :], in0=mean_var[:, tiles, 1:2], in1=neg_half[:], op=ALU.pow)

        def shifts(g):
            tiles = slice(g * GROUP, (g + 1) * GROUP)
            nc.vector.scalar_tensor_tensor(
                out=shift[:, tiles, :],
                in0=mean_var[:, tiles, 0:1],
                scalar=-1.0,
                in1=rstd[:, tiles, :],
                op0=ALU.mult,
                op1=ALU.mult,
            )

        def norm_engines(g):
            if g < NORM_AHEAD:
                return FIRST_NORM_ENGINES
            return NORM_ENGINES if g + STATS_AHEAD < N_GROUPS + NORM_AHEAD else LAST_NORM_ENGINES

        def new_u():
            return u_pool.tile([P, GROUP, PACK, P], F32, name="u")

        def normalise(g, engine):
            for i in range(GROUP):
                at = g * GROUP + i
                owner = norm_engines(g)[i]
                parts = (
                    (owner, x_tiles[g][:, i, :], slice(0, RAW_PARTS)),
                    ("scalar" if owner == "gpsimd" else owner, feat[:, :, at], slice(RAW_PARTS, P)),
                )
                for worker, source, place in parts:
                    if worker != engine:
                        continue
                    source = source.rearrange("r (p t) -> r t p", t=PACK)
                    result = u_tiles[g][:, i, :, place]
                    if engine == "scalar":
                        nc.scalar.activation(
                            out=result, in_=source, func=ACT.Identity, scale=rstd[:, at, :], bias=shift[:, at, :]
                        )
                    else:
                        (nc.vector if engine == "vector" else nc.gpsimd).tensor_scalar(
                            out=result,
                            in0=source,
                            scalar1=rstd[:, at, :],
                            scalar2=shift[:, at, :],
                            op0=ALU.mult,
                            op1=ALU.add,
                        )

        def transpose(g):
            banks = []
            for t in range(PACK):
                tp = psum_t.tile([P, GROUP * P], F32, name="tp")
                for i in range(GROUP):
                    nc.tensor.transpose(tp[:, i * P : (i + 1) * P], u_tiles[g][:, i, t, :], identity[:])
                banks.append(tp)
            return banks

        def scale(g, engine):
            kind = g // GROUPS
            on_vector = LAST_BANKS_ON_VECTOR if g + STATS_AHEAD >= N_GROUPS else 0
            for t in range(PACK):
                gamma = col[:, 2 * kind, t : t + 1]
                beta = col[:, 2 * kind + 1, t : t + 1]
                result = plane_tiles[g][:, t, :]
                if engine == "scalar" and t < PACK - on_vector:
                    nc.scalar.activation(out=result, in_=bank_tiles[g][t][:], func=ACT.Identity, scale=gamma, bias=beta)
                if engine == "vector" and t >= PACK - on_vector:
                    nc.vector.tensor_scalar(
                        out=result, in0=bank_tiles[g][t][:], scalar1=gamma, scalar2=beta, op0=ALU.mult, op1=ALU.add
                    )

        def regroup(g):
            grouped = q_pool.tile([P, GROUP * P, PACK], BF16, name="grouped", align_bytes=64)
            nc.vector.tensor_copy(
                out=grouped[:].rearrange("p (c i) t -> p c t i", i=4),
                in_=plane_tiles[g][:].rearrange("p t (c i) -> p c t i", i=4),
            )
            return grouped

        def quantise(g):
            codes = q_pool.tile([P, GROUP * P], U32, name="codes", align_bytes=64)
            scales = q_pool.tile([P, GROUP * P], U8, name="scales", align_bytes=64)
            nc.vector.quantize_mx(
                out=codes[:].bitcast(FP8X4), scales=scales[:], in_=grouped_tiles[g][:].rearrange("p r t -> p (r t)")
            )
            return codes, scales

        def project(g):
            kind = g // GROUPS
            codes, scales = quantised[g]
            w_codes, w_scales = w_quantised[kind]
            accs = []
            for pair in range(GROUP // 2):
                acc = psum_o.tile([P, 2, D_OUT], F32, name="acc")
                for i in range(2):
                    rows = slice((2 * pair + i) * P, (2 * pair + i + 1) * P)
                    nc.tensor.matmul_mx(
                        out=acc[:, i, :],
                        lhsT=codes[:, rows].bitcast(FP8X4),
                        lhsT_scale=scales[:, rows],
                        rhs=w_codes[:].bitcast(FP8X4),
                        rhs_scale=w_scales[:],
                        start=True,
                        stop=True,
                    )
                accs.append(acc)
            return accs

        def gelu_and_store(g):
            kind, first = divmod(g, GROUPS)
            first *= GROUP
            o_sb = o_pool.tile([P, GROUP, D_OUT], F32, name="o_sb")
            for pair in range(GROUP // 2):
                nc.scalar.activation(out=o_sb[:, 2 * pair : 2 * pair + 2, :], in_=acc_tiles[g][pair][:], func=ACT.Gelu)
            out_rows = out[kind].rearrange("(p t) d -> p t d", t=TILES)
            nc.sync.dma_start(out=out_rows[:, first : first + GROUP, :], in_=o_sb[:])

        u_tiles = {}
        bank_tiles = {}
        plane_tiles = {}
        grouped_tiles = {}
        quantised = {}
        acc_tiles = {}

        def round_of(n):
            last, this, ahead, new = n - 1, n, n + NORM_AHEAD, n + STATS_AHEAD
            if ahead < N_GROUPS:
                shifts(ahead)
            if 0 <= last:
                grouped_tiles[last] = regroup(last)
            if 0 <= this < N_GROUPS:
                plane_tiles[this] = q_pool.tile([P, PACK, GROUP * P], BF16, name="planes")
                scale(this, "scalar")
            if ahead < N_GROUPS:
                u_tiles[ahead] = new_u()
                normalise(ahead, "vector")
            if 0 <= last:
                quantised[last] = quantise(last)
                acc_tiles[last] = project(last)
            if new - 1 < N_GROUPS:
                aggregate(new - 1)
                inverse_roots(new - 1)
            if ahead < N_GROUPS:
                normalise(ahead, "gpsimd")
                normalise(ahead, "scalar")
            if 0 <= this < N_GROUPS:
                scale(this, "vector")
            if 0 <= this + 1 < N_GROUPS:
                bank_tiles[this + 1] = transpose(this + 1)
            if 0 <= last:
                gelu_and_store(last)
            if new < N_GROUPS:
                statistics(new)
            if n + LOAD_AHEAD < N_GROUPS:
                x_tiles[n + LOAD_AHEAD] = load_group(n + LOAD_AHEAD)

        early = slice(0, EARLY_TILES)
        late = slice(EARLY_TILES, ALL_TILES)
        early_halves = new_half("early_feat", early), new_half("early_sq", early)
        late_halves = new_half("late_feat", late), new_half("late_sq", late)
        t2v_arguments(early)
        t2v_fold(early)
        t2v_sines(early)
        t2v_squares(early)
        t2v_sum(feat, early, early_halves[0], halvings)
        t2v_sum(squares, early, early_halves[1], halvings)
        statistics(0)
        t2v_arguments(late)
        t2v_fold(late)
        t2v_tuples(early, *early_halves)
        aggregate(0)
        inverse_roots(0)
        grouped_w = [regroup_weights(kind) for kind in range(KINDS)]
        t2v_sines(late)
        statistics(1)

        round_of(-2)
        t2v_squares(late)
        col = keep.tile([P, len(column_vectors), PACK], F32, name="col")
        nc.vector.tensor_copy(out=col[:], in_=vec_bf[:, :, 0:PACK])
        round_of(-1)
        w_quantised = [quantise_weights(kind, grouped_w[kind]) for kind in range(KINDS)]
        late_pieces = [
            (source, half, steps)
            for steps in (halvings[:1], halvings[1:])
            for source, half in zip((feat, squares), late_halves)
        ]
        for n in range(N_GROUPS + 1):
            if n == len(late_pieces):
                t2v_tuples(late, *late_halves)
            round_of(n)
            if n < len(late_pieces):
                source, half, steps = late_pieces[n]
                t2v_sum(source, late, half, steps)
